import numpy as np
import ml_dtypes


def mxq(x, axis, fmt="e4m3"):
    dtype, down = {"e4m3": (ml_dtypes.float8_e4m3fn, 7), "e5m2": (ml_dtypes.float8_e5m2, 14)}[fmt]
    v = np.moveaxis(np.asarray(x, np.float32).astype(ml_dtypes.bfloat16).astype(np.float64), axis, -1)
    blocks = v.reshape(v.shape[:-1] + (-1, 32))
    amax = np.abs(blocks).max(-1, keepdims=True)
    byte = np.maximum(np.where(amax > 0, np.frexp(amax)[1] - 1 + 127, 0) - down, 1)
    scale = np.exp2(byte - 127.0)
    codes = (blocks / scale).astype(np.float32).astype(dtype).astype(np.float64)
    return np.moveaxis((codes * scale).reshape(v.shape), -1, axis)


BF16 = ml_dtypes.bfloat16


def bf(x):
    return np.asarray(x, np.float32).astype(BF16)


def f64(x):
    return np.asarray(x).astype(np.float64)


B, C, U, H, W, KB, R, Q0 = 6, 16, 4, 256, 8, 512, 4, 128
S, D = H * U, C * U * W
SQ = S - Q0
EPS = 1e-12
NEG = -1e15


def l2norm(x):
    n = np.sqrt((x * x).sum(-1, keepdims=True))
    return x / np.maximum(n, EPS)


def mix(coef, dirs):
    return (coef[:, :, :, None] * dirs).sum(2) / np.sqrt(R)


def setup_inputs():
    dirs = np.random.standard_normal((R, D))
    vdirs = np.random.standard_normal((R, D))
    a = np.random.standard_normal((B, SQ, R))
    b = np.random.standard_normal((B, S, R))
    q = mix(a, dirs) + 0.3 * np.random.standard_normal((B, SQ, D))
    k = mix(b, dirs) + 0.3 * np.random.standard_normal((B, S, D))
    v = mix(b, vdirs) + 0.5 * np.random.standard_normal((B, S, D))
    return {"q_rows": bf(q), "k_rows": bf(k), "v_rows": bf(v)}


def reference(q_rows, k_rows, v_rows):
    v = f64(v_rows)
    qn = mxq(l2norm(f64(q_rows)), 2, "e4m3")
    kn = mxq(l2norm(f64(k_rows)), 2, "e4m3")
    vq = mxq(v, 1, "e4m3")
    causal = np.tril(np.ones((S, S), dtype=bool))
    out = []
    for i in range(0, S, KB):
        j = i + KB
        lo = max(i, Q0)
        att = qn[:, lo - Q0:j - Q0] @ kn[:, :j].transpose(0, 2, 1)
        att = np.where(causal[lo:j, :j], att, NEG)
        e = np.exp(att - att.max(-1, keepdims=True))
        out.append((mxq(e, 2, "e4m3") @ vq[:, :j]) / e.sum(-1, keepdims=True))
    return np.concatenate(out, 1) + v[:, Q0:]

@@ -1,0 +1,293 @@
+from contextlib import ExitStack
+
+import concourse.mybir as mybir
+from concourse.masks import make_identity
+
+BF16 = mybir.dt.bfloat16
+F32 = mybir.dt.float32
+U32 = mybir.dt.uint32
+U8 = mybir.dt.uint8
+FP8X4 = mybir.dt.float8_e4m3fn_x4
+ALU = mybir.AluOpType
+ACT = mybir.ActivationFunctionType
+AXIS = mybir.AxisListType
+
+P = 128
+PACK = 4
+K_PASS = P * PACK
+BANK = 512
+BATCHES = 6
+FEATURES = 512
+KEYS = 1024
+FIRST_QUERY = 128
+QUERIES = KEYS - FIRST_QUERY
+QUERY_TILES = QUERIES // P
+PAIR = 2
+PARTS = KEYS // (PAIR * P)
+EPS = 1e-12
+NEG = -1e15
+
+FLOPS = 2 * 2 * BATCHES * FEATURES * (384 * 512 + 512 * 1024)
+
+
+def mx_widths(width):
+    pieces = []
+    start = 0
+    for n in (512, 256, 128):
+        while width - start >= n:
+            pieces.append((start, n))
+            start += n
+    return pieces
+
+
+def tile_spatialangularattention_pa_t_kernel(tc, q_rows, k_rows, v_rows, out):
+    nc = tc.nc
+    with ExitStack() as stack:
+        const = stack.enter_context(tc.tile_pool(name="const", bufs=1))
+        row_pool = stack.enter_context(tc.tile_pool(name="rows", bufs=3))
+        value_pool = stack.enter_context(tc.tile_pool(name="values", bufs=2))
+        batch_pool = stack.enter_context(tc.tile_pool(name="batch", bufs=2))
+        stat_pool = stack.enter_context(tc.tile_pool(name="stats", bufs=4))
+        work_pool = stack.enter_context(tc.tile_pool(name="work", bufs=3))
+        flip_psum = stack.enter_context(tc.psum_pool(name="flip_psum", bufs=2))
+        score_psum = stack.enter_context(tc.psum_pool(name="score_psum", bufs=4))
+        e_psum = stack.enter_context(tc.psum_pool(name="e_psum", bufs=1))
+        out_psum = stack.enter_context(tc.psum_pool(name="out_psum", bufs=1))
+
+        identity = const.tile([P, P], F32)
+        make_identity(nc, identity[:])
+        causal = const.tile([P, P], F32)
+        nc.gpsimd.memset(causal[:], 0.0)
+        nc.gpsimd.affine_select(
+            out=causal[:],
+            in_=causal[:],
+            pattern=[[-1, P]],
+            compare_op=ALU.is_ge,
+            fill=NEG,
+            base=0,
+            channel_multiplier=1,
+        )
+        minus_half = const.tile([P, PAIR], F32)
+        nc.vector.memset(minus_half[:], -0.5)
+
+        e_rows = []
+        for qi in range(QUERY_TILES):
+            seen = (qi + 2) * P
+            reach = K_PASS if seen <= K_PASS else KEYS
+            e_tile = const.tile([P, reach], BF16, name="e_rows%d" % qi)
+            if seen < reach:
+                nc.vector.memset(e_tile[:, seen:], 0.0)
+            e_rows.append(e_tile)
+
+        def normalise_and_quantise(rows, tiles, codes, scales):
+            raw = row_pool.tile([P, PAIR, FEATURES], BF16)
+            nc.sync.dma_start(out=raw[:, :tiles, :], in_=rows.rearrange("(t p) d -> p t d", p=P))
+            unit = row_pool.tile([P, PAIR, FEATURES], BF16)
+            square_sum = stat_pool.tile([P, PAIR], F32)
+            for t in range(tiles):
+                nc.scalar.activation(
+                    out=unit[:, t, :],
+                    in_=raw[:, t, :],
+                    func=ACT.Square,
+                    accum_out=square_sum[:, t : t + 1],
+                )
+            floored = stat_pool.tile([P, PAIR], F32)
+            nc.gpsimd.tensor_scalar_max(
+                out=floored[:, :tiles], in0=square_sum[:, :tiles], scalar1=EPS * EPS
+            )
+            inv_norm = stat_pool.tile([P, PAIR], F32)
+            nc.gpsimd.tensor_tensor(
+                out=inv_norm[:, :tiles],
+                in0=floored[:, :tiles],
+                in1=minus_half[:, :tiles],
+                op=ALU.pow,
+            )
+            for t in range(tiles):
+                nc.vector.tensor_scalar_mul(
+                    out=unit[:, t, :], in0=raw[:, t, :], scalar1=inv_norm[:, t : t + 1]
+                )
+            flipped = flip_psum.tile([P, PAIR, 2, P], F32)
+            for t in range(tiles):
+                words = unit[:, t, :].bitcast(F32)
+                for u in range(2):
+                    nc.tensor.transpose(
+                        flipped[:, t, u, :], words[:, u * P : (u + 1) * P], identity[:]
+                    )
+            grouped = row_pool.tile([P, PAIR * FEATURES], BF16, align_bytes=64)
+            grouped_words = grouped[:].bitcast(F32).rearrange("p (t r u) -> p t r u", t=PAIR, u=2)
+            nc.scalar.copy(
+                out=grouped_words[:, :tiles],
+                in_=flipped[:, :tiles].rearrange("p t u r -> p t r u"),
+            )
+            nc.vector.quantize_mx(
+                out=codes.bitcast(FP8X4), scales=scales, in_=grouped[:, : tiles * FEATURES]
+            )
+
+        def load_and_quantise_values(b, g, batch):
+            first = g * K_PASS
+            raw = value_pool.tile([P, PACK, FEATURES], BF16)
+            nc.sync.dma_start(
+                out=raw[:].rearrange("p (u e) d -> p u e d", e=2),
+                in_=v_rows[b, first : first + K_PASS, :].rearrange("(u p e) d -> p u e d", p=P, e=2),
+            )
+            skip = max(FIRST_QUERY - first, 0) // P
+            nc.sync.dma_start(
+                out=batch["residual"][:, g * PACK + skip : (g + 1) * PACK, :],
+                in_=v_rows[b, first + skip * P : first + K_PASS, :].rearrange(
+                    "(j p) d -> p j d", p=P
+                ),
+            )
+            grouped = value_pool.tile([P, FEATURES, PACK], BF16, align_bytes=64)
+            nc.vector.tensor_copy(
+                out=grouped[:].rearrange("p (c i) s -> p c s i", i=4),
+                in_=raw[:].rearrange("p s (c i) -> p c s i", i=4),
+            )
+            columns = slice(g * FEATURES, (g + 1) * FEATURES)
+            nc.vector.quantize_mx(
+                out=batch["v_codes"][:, columns].bitcast(FP8X4),
+                scales=batch["v_scales"][:, columns],
+                in_=grouped[:].rearrange("p d s -> p (d s)"),
+            )
+
+        def open_batch():
+            q_codes = batch_pool.tile([P, QUERIES], U32, align_bytes=64)
+            q_scales = batch_pool.tile([P, QUERIES], U8, align_bytes=64)
+            k_codes = batch_pool.tile([P, KEYS], U32, align_bytes=64)
+            k_scales = batch_pool.tile([P, KEYS], U8, align_bytes=64)
+            v_codes = batch_pool.tile([P, 2 * FEATURES], U32, align_bytes=64)
+            v_scales = batch_pool.tile([P, 2 * FEATURES], U8, align_bytes=64)
+            residual = batch_pool.tile([P, KEYS // P, FEATURES], BF16)
+            return {
+                "q_codes": q_codes,
+                "q_scales": q_scales,
+                "k_codes": k_codes,
+                "k_scales": k_scales,
+                "v_codes": v_codes,
+                "v_scales": v_scales,
+                "residual": residual,
+            }
+
+        def prepare(b, part, batch):
+            first = part * PAIR * P
+            rows = slice(first, first + PAIR * P)
+            normalise_and_quantise(
+                k_rows[b, rows, :], PAIR, batch["k_codes"][:, rows], batch["k_scales"][:, rows]
+            )
+            tiles = min(PAIR, QUERY_TILES - part * PAIR)
+            rows = slice(first, first + tiles * P)
+            normalise_and_quantise(
+                q_rows[b, rows, :], tiles, batch["q_codes"][:, rows], batch["q_scales"][:, rows]
+            )
+            if part < KEYS // K_PASS:
+                load_and_quantise_values(b, part, batch)
+
+        def attend(b, qi, batch):
+            seen = (qi + 2) * P
+            passes = e_rows[qi].shape[1] // K_PASS
+            queries = slice(qi * P, (qi + 1) * P)
+
+            scores = []
+            for first in range(0, seen, BANK):
+                bank = score_psum.tile([P, BANK], F32)
+                for start, n in mx_widths(min(seen - first, BANK)):
+                    keys = slice(first + start, first + start + n)
+                    nc.tensor.matmul_mx(
+                        out=bank[:, start : start + n],
+                        lhsT=batch["q_codes"][:, queries].bitcast(FP8X4),
+                        lhsT_scale=batch["q_scales"][:, queries],
+                        rhs=batch["k_codes"][:, keys].bitcast(FP8X4),
+                        rhs_scale=batch["k_scales"][:, keys],
+                        start=True,
+                        stop=True,
+                    )
+                scores.append(bank)
+
+            masked = work_pool.tile([P, P], F32)
+            diagonal = (seen - P) % BANK
+            nc.vector.tensor_tensor(
+                out=masked[:], in0=scores[-1][:, diagonal : diagonal + P], in1=causal[:], op=ALU.add
+            )
+            pieces = []
+            for g, bank in enumerate(scores):
+                open_keys = min(seen - P - g * BANK, BANK)
+                if open_keys > 0:
+                    pieces.append((g * BANK, bank[:, :open_keys]))
+            pieces.append((seen - P, masked[:]))
+
+            piece_max = stat_pool.tile([P, 3], F32)
+            for j, (first, piece) in enumerate(pieces):
+                nc.vector.tensor_reduce(
+                    out=piece_max[:, j : j + 1], in_=piece, axis=AXIS.X, op=ALU.max
+                )
+            minus_max = stat_pool.tile([P, 1], F32)
+            nc.vector.tensor_reduce(
+                out=minus_max[:], in_=piece_max[:, : len(pieces)], axis=AXIS.X, op=ALU.max, negate=True
+            )
+
+            piece_sum = stat_pool.tile([P, 3], F32)
+            for j, (first, piece) in enumerate(pieces):
+                nc.scalar.activation(
+                    out=e_rows[qi][:, first : first + piece.shape[1]],
+                    in_=piece,
+                    func=ACT.Exp,
+                    bias=minus_max[:, 0:1],
+                    scale=1.0,
+                    accum_out=piece_sum[:, j : j + 1],
+                )
+            row_sum = stat_pool.tile([P, 1], F32)
+            nc.vector.tensor_reduce(
+                out=row_sum[:], in_=piece_sum[:, : len(pieces)], axis=AXIS.X, op=ALU.add
+            )
+            inv_sum = stat_pool.tile([P, 1], F32)
+            nc.vector.reciprocal(out=inv_sum[:], in_=row_sum[:])
+
+            flipped = e_psum.tile([P, 2 * (KEYS // K_PASS), P], F32)
+            e_words = e_rows[qi][:].bitcast(F32)
+            for w in range(2 * passes):
+                nc.tensor.transpose(flipped[:, w, :], e_words[:, w * P : (w + 1) * P], identity[:])
+            grouped = work_pool.tile([P, KEYS // K_PASS * K_PASS], BF16, align_bytes=64)
+            grouped_words = grouped[:].bitcast(F32).rearrange("p (g i u) -> p g i u", i=P, u=2)
+            nc.scalar.copy(
+                out=grouped_words[:, :passes],
+                in_=flipped[:, : 2 * passes, :].rearrange("p (g u) i -> p g i u", u=2),
+            )
+            e_codes = work_pool.tile([P, KEYS // K_PASS * P], U32, align_bytes=64)
+            e_scales = work_pool.tile([P, KEYS // K_PASS * P], U8, align_bytes=64)
+            nc.vector.quantize_mx(
+                out=e_codes[:, : passes * P].bitcast(FP8X4),
+                scales=e_scales[:, : passes * P],
+                in_=grouped[:, : passes * K_PASS],
+            )
+
+            mixed = out_psum.tile([P, FEATURES], F32)
+            for g in range(passes):
+                nc.tensor.matmul_mx(
+                    out=mixed[:],
+                    lhsT=e_codes[:, g * P : (g + 1) * P].bitcast(FP8X4),
+                    lhsT_scale=e_scales[:, g * P : (g + 1) * P],
+                    rhs=batch["v_codes"][:, g * FEATURES : (g + 1) * FEATURES].bitcast(FP8X4),
+                    rhs_scale=batch["v_scales"][:, g * FEATURES : (g + 1) * FEATURES],
+                    start=(g == 0),
+                    stop=(g == passes - 1),
+                )
+            result = work_pool.tile([P, FEATURES], F32)
+            nc.vector.scalar_tensor_tensor(
+                out=result[:],
+                in0=mixed[:],
+                scalar=inv_sum[:, 0:1],
+                in1=batch["residual"][:, qi + FIRST_QUERY // P, :],
+                op0=ALU.mult,
+                op1=ALU.add,
+            )
+            nc.sync.dma_start(out=out[b, queries, :], in_=result[:])
+
+        batch = open_batch()
+        for part in range(PARTS):
+            prepare(0, part, batch)
+        for b in range(BATCHES):
+            following = open_batch() if b + 1 < BATCHES else None
+            for qi in range(QUERY_TILES):
+                attend(b, qi, batch)
+                if following is not None and qi < PARTS:
+                    prepare(b + 1, qi, following)
+            batch = following

@@ -22,10 +22,15 @@ KEYS = 1024
 FIRST_QUERY = 128
 QUERIES = KEYS - FIRST_QUERY
 QUERY_TILES = QUERIES // P
+TILES = BATCHES * QUERY_TILES
 PAIR = 2
-PARTS = KEYS // (PAIR * P)
 EPS = 1e-12
 NEG = -1e15
+
+LOAD_AHEAD = 6
+SQUARE_AHEAD = 4
+FLIP_AHEAD = 3
+QUANTISE_AHEAD = 2
 
 FLOPS = 2 * 2 * BATCHES * FEATURES * (384 * 512 + 512 * 1024)
 
@@ -40,11 +45,21 @@ def mx_widths(width):
     return pieces
 
 
+def groups_due(n):
+    if not 0 <= n < TILES:
+        return []
+    b, qi = divmod(n, QUERY_TILES)
+    if qi == 0:
+        return [(b, 0), (b, 1)]
+    return [(b, qi + 1)]
+
+
 def tile_spatialangularattention_pa_t_kernel(tc, q_rows, k_rows, v_rows, out):
     nc = tc.nc
     with ExitStack() as stack:
         const = stack.enter_context(tc.tile_pool(name="const", bufs=1))
-        row_pool = stack.enter_context(tc.tile_pool(name="rows", bufs=3))
+        raw_pool = stack.enter_context(tc.tile_pool(name="raw", bufs=6))
+        row_pool = stack.enter_context(tc.tile_pool(name="rows", bufs=4))
         value_pool = stack.enter_context(tc.tile_pool(name="values", bufs=2))
         batch_pool = stack.enter_context(tc.tile_pool(name="batch", bufs=2))
         stat_pool = stack.enter_context(tc.tile_pool(name="stats", bufs=4))
@@ -53,6 +68,7 @@ def tile_spatialangularattention_pa_t_kernel(tc, q_rows, k_rows, v_rows, out):
         score_psum = stack.enter_context(tc.psum_pool(name="score_psum", bufs=4))
         e_psum = stack.enter_context(tc.psum_pool(name="e_psum", bufs=1))
         out_psum = stack.enter_context(tc.psum_pool(name="out_psum", bufs=1))
+        stack.enter_context(tc.manual_schedule())
 
         identity = const.tile([P, P], F32)
         make_identity(nc, identity[:])
@@ -79,77 +95,12 @@ def tile_spatialangularattention_pa_t_kernel(tc, q_rows, k_rows, v_rows, out):
                 nc.vector.memset(e_tile[:, seen:], 0.0)
             e_rows.append(e_tile)
 
-        def normalise_and_quantise(rows, tiles, codes, scales):
-            raw = row_pool.tile([P, PAIR, FEATURES], BF16)
-            nc.sync.dma_start(out=raw[:, :tiles, :], in_=rows.rearrange("(t p) d -> p t d", p=P))
-            unit = row_pool.tile([P, PAIR, FEATURES], BF16)
-            square_sum = stat_pool.tile([P, PAIR], F32)
-            for t in range(tiles):
-                nc.scalar.activation(
-                    out=unit[:, t, :],
-                    in_=raw[:, t, :],
-                    func=ACT.Square,
-                    accum_out=square_sum[:, t : t + 1],
-                )
-            floored = stat_pool.tile([P, PAIR], F32)
-            nc.gpsimd.tensor_scalar_max(
-                out=floored[:, :tiles], in0=square_sum[:, :tiles], scalar1=EPS * EPS
-            )
-            inv_norm = stat_pool.tile([P, PAIR], F32)
-            nc.gpsimd.tensor_tensor(
-                out=inv_norm[:, :tiles],
-                in0=floored[:, :tiles],
-                in1=minus_half[:, :tiles],
-                op=ALU.pow,
-            )
-            for t in range(tiles):
-                nc.vector.tensor_scalar_mul(
-                    out=unit[:, t, :], in0=raw[:, t, :], scalar1=inv_norm[:, t : t + 1]
-                )
-            flipped = flip_psum.tile([P, PAIR, 2, P], F32)
-            for t in range(tiles):
-                words = unit[:, t, :].bitcast(F32)
-                for u in range(2):
-                    nc.tensor.transpose(
-                        flipped[:, t, u, :], words[:, u * P : (u + 1) * P], identity[:]
-                    )
-            grouped = row_pool.tile([P, PAIR * FEATURES], BF16, align_bytes=64)
-            grouped_words = grouped[:].bitcast(F32).rearrange("p (t r u) -> p t r u", t=PAIR, u=2)
-            nc.scalar.copy(
-                out=grouped_words[:, :tiles],
-                in_=flipped[:, :tiles].rearrange("p t u r -> p t r u"),
-            )
-            nc.vector.quantize_mx(
-                out=codes.bitcast(FP8X4), scales=scales, in_=grouped[:, : tiles * FEATURES]
-            )
+        batches = {}
+        groups = {}
+        tiles = {}
 
-        def load_and_quantise_values(b, g, batch):
-            first = g * K_PASS
-            raw = value_pool.tile([P, PACK, FEATURES], BF16)
-            nc.sync.dma_start(
-                out=raw[:].rearrange("p (u e) d -> p u e d", e=2),
-                in_=v_rows[b, first : first + K_PASS, :].rearrange("(u p e) d -> p u e d", p=P, e=2),
-            )
-            skip = max(FIRST_QUERY - first, 0) // P
-            nc.sync.dma_start(
-                out=batch["residual"][:, g * PACK + skip : (g + 1) * PACK, :],
-                in_=v_rows[b, first + skip * P : first + K_PASS, :].rearrange(
-                    "(j p) d -> p j d", p=P
-                ),
-            )
-            grouped = value_pool.tile([P, FEATURES, PACK], BF16, align_bytes=64)
-            nc.vector.tensor_copy(
-                out=grouped[:].rearrange("p (c i) s -> p c s i", i=4),
-                in_=raw[:].rearrange("p s (c i) -> p c s i", i=4),
-            )
-            columns = slice(g * FEATURES, (g + 1) * FEATURES)
-            nc.vector.quantize_mx(
-                out=batch["v_codes"][:, columns].bitcast(FP8X4),
-                scales=batch["v_scales"][:, columns],
-                in_=grouped[:].rearrange("p d s -> p (d s)"),
-            )
 
-        def open_batch():
+        def open_batch(b):
             q_codes = batch_pool.tile([P, QUERIES], U32, align_bytes=64)
             q_scales = batch_pool.tile([P, QUERIES], U8, align_bytes=64)
             k_codes = batch_pool.tile([P, KEYS], U32, align_bytes=64)
@@ -157,7 +108,7 @@ def tile_spatialangularattention_pa_t_kernel(tc, q_rows, k_rows, v_rows, out):
             v_codes = batch_pool.tile([P, 2 * FEATURES], U32, align_bytes=64)
             v_scales = batch_pool.tile([P, 2 * FEATURES], U8, align_bytes=64)
             residual = batch_pool.tile([P, KEYS // P, FEATURES], BF16)
-            return {
+            batches[b] = {
                 "q_codes": q_codes,
                 "q_scales": q_scales,
                 "k_codes": k_codes,
@@ -167,32 +118,146 @@ def tile_spatialangularattention_pa_t_kernel(tc, q_rows, k_rows, v_rows, out):
                 "residual": residual,
             }
 
-        def prepare(b, part, batch):
-            first = part * PAIR * P
-            rows = slice(first, first + PAIR * P)
-            normalise_and_quantise(
-                k_rows[b, rows, :], PAIR, batch["k_codes"][:, rows], batch["k_scales"][:, rows]
+        def load_rows(group):
+            b, j = group
+            if j == 0:
+                open_batch(b)
+            first = (j // 2) * PAIR * P
+            source, kind, total = (k_rows, "k", KEYS) if j % 2 == 0 else (q_rows, "q", QUERIES)
+            count = min(PAIR, (total - first) // P)
+            rows = slice(first, first + count * P)
+            raw = raw_pool.tile([P, PAIR, FEATURES], BF16)
+            nc.sync.dma_start(
+                out=raw[:, :count, :], in_=source[b, rows, :].rearrange("(t p) d -> p t d", p=P)
             )
-            tiles = min(PAIR, QUERY_TILES - part * PAIR)
-            rows = slice(first, first + tiles * P)
-            normalise_and_quantise(
-                q_rows[b, rows, :], tiles, batch["q_codes"][:, rows], batch["q_scales"][:, rows]
-            )
-            if part < KEYS // K_PASS:
-                load_and_quantise_values(b, part, batch)
+            groups[group] = {
+                "raw": raw,
+                "count": count,
+                "codes": batches[b][kind + "_codes"][:, rows],
+                "scales": batches[b][kind + "_scales"][:, rows],
+            }
+            if j % 4 == 1:
+                load_values(group)
 
-        def attend(b, qi, batch):
+        def load_values(group):
+            b, j = group
+            g = j // 4
+            first = g * K_PASS
+            raw_values = value_pool.tile([P, PACK, FEATURES], BF16)
+            nc.sync.dma_start(
+                out=raw_values[:].rearrange("p (u e) d -> p u e d", e=2),
+                in_=v_rows[b, first : first + K_PASS, :].rearrange("(u p e) d -> p u e d", p=P, e=2),
+            )
+            groups[group]["raw_values"] = raw_values
+            skip = max(FIRST_QUERY - first, 0) // P
+            nc.sync.dma_start(
+                out=batches[b]["residual"][:, g * PACK + skip : (g + 1) * PACK, :],
+                in_=v_rows[b, first + skip * P : first + K_PASS, :].rearrange(
+                    "(t p) d -> p t d", p=P
+                ),
+            )
+
+        def square_sums(group):
+            state = groups[group]
+            count = state["count"]
+            unit = row_pool.tile([P, PAIR, FEATURES], BF16)
+            square_sum = stat_pool.tile([P, PAIR], F32)
+            for t in range(count):
+                nc.scalar.activation(
+                    out=unit[:, t, :],
+                    in_=state["raw"][:, t, :],
+                    func=ACT.Square,
+                    accum_out=square_sum[:, t : t + 1],
+                )
+            floored = stat_pool.tile([P, PAIR], F32)
+            nc.gpsimd.tensor_scalar_max(
+                out=floored[:, :count], in0=square_sum[:, :count], scalar1=EPS * EPS
+            )
+            inv_norm = stat_pool.tile([P, PAIR], F32)
+            nc.gpsimd.tensor_tensor(
+                out=inv_norm[:, :count],
+                in0=floored[:, :count],
+                in1=minus_half[:, :count],
+                op=ALU.pow,
+            )
+            state["unit"] = unit
+            state["inv_norm"] = inv_norm
+
+        def normalise(group):
+            state = groups[group]
+            for t in range(state["count"]):
+                nc.vector.tensor_scalar_mul(
+                    out=state["unit"][:, t, :],
+                    in0=state["raw"][:, t, :],
+                    scalar1=state["inv_norm"][:, t : t + 1],
+                )
+
+        def flip_rows(group):
+            state = groups[group]
+            flipped = flip_psum.tile([P, PAIR, 2, P], F32)
+            for t in range(state["count"]):
+                words = state["unit"][:, t, :].bitcast(F32)
+                for u in range(2):
+                    nc.tensor.transpose(
+                        flipped[:, t, u, :], words[:, u * P : (u + 1) * P], identity[:]
+                    )
+            state["flipped"] = flipped
+
+        def copy_rows(group):
+            state = groups[group]
+            count = state["count"]
+            grouped = row_pool.tile([P, PAIR * FEATURES], BF16, align_bytes=64)
+            grouped_words = grouped[:].bitcast(F32).rearrange("p (t r u) -> p t r u", t=PAIR, u=2)
+            nc.scalar.copy(
+                out=grouped_words[:, :count],
+                in_=state["flipped"][:, :count].rearrange("p t u r -> p t r u"),
+            )
+            state["grouped"] = grouped
+
+        def quantise_rows(group):
+            state = groups[group]
+            nc.vector.quantize_mx(
+                out=state["codes"].bitcast(FP8X4),
+                scales=state["scales"],
+                in_=state["grouped"][:, : state["count"] * FEATURES],
+            )
+
+        def regroup_values(group):
+            if "raw_values" not in groups[group]:
+                return
+            grouped_values = value_pool.tile([P, FEATURES, PACK], BF16, align_bytes=64)
+            nc.vector.tensor_copy(
+                out=grouped_values[:].rearrange("p (c i) s -> p c s i", i=4),
+                in_=groups[group]["raw_values"][:].rearrange("p s (c i) -> p c s i", i=4),
+            )
+            groups[group]["grouped_values"] = grouped_values
+
+        def quantise_values(group):
+            if "raw_values" not in groups[group]:
+                return
+            b, j = group
+            columns = slice((j // 4) * FEATURES, (j // 4 + 1) * FEATURES)
+            nc.vector.quantize_mx(
+                out=batches[b]["v_codes"][:, columns].bitcast(FP8X4),
+                scales=batches[b]["v_scales"][:, columns],
+                in_=groups[group]["grouped_values"][:].rearrange("p d s -> p (d s)"),
+            )
+
+
+        def score(n):
+            if not 0 <= n < TILES:
+                return
+            b, qi = divmod(n, QUERY_TILES)
+            batch = batches[b]
             seen = (qi + 2) * P
-            passes = e_rows[qi].shape[1] // K_PASS
             queries = slice(qi * P, (qi + 1) * P)
-
-            scores = []
+            banks = []
             for first in range(0, seen, BANK):
                 bank = score_psum.tile([P, BANK], F32)
-                for start, n in mx_widths(min(seen - first, BANK)):
-                    keys = slice(first + start, first + start + n)
+                for start, width in mx_widths(min(seen - first, BANK)):
+                    keys = slice(first + start, first + start + width)
                     nc.tensor.matmul_mx(
-                        out=bank[:, start : start + n],
+                        out=bank[:, start : start + width],
                         lhsT=batch["q_codes"][:, queries].bitcast(FP8X4),
                         lhsT_scale=batch["q_scales"][:, queries],
                         rhs=batch["k_codes"][:, keys].bitcast(FP8X4),
@@ -200,94 +265,181 @@ def tile_spatialangularattention_pa_t_kernel(tc, q_rows, k_rows, v_rows, out):
                         start=True,
                         stop=True,
                     )
-                scores.append(bank)
+                banks.append(bank)
+            tiles[n] = {"batch": batch, "b": b, "qi": qi, "seen": seen, "banks": banks}
 
+        def piece_maxima(n):
+            if not 0 <= n < TILES:
+                return
+            state = tiles[n]
+            seen = state["seen"]
             masked = work_pool.tile([P, P], F32)
             diagonal = (seen - P) % BANK
             nc.vector.tensor_tensor(
-                out=masked[:], in0=scores[-1][:, diagonal : diagonal + P], in1=causal[:], op=ALU.add
+                out=masked[:],
+                in0=state["banks"][-1][:, diagonal : diagonal + P],
+                in1=causal[:],
+                op=ALU.add,
             )
             pieces = []
-            for g, bank in enumerate(scores):
+            for g, bank in enumerate(state["banks"]):
                 open_keys = min(seen - P - g * BANK, BANK)
                 if open_keys > 0:
                     pieces.append((g * BANK, bank[:, :open_keys]))
             pieces.append((seen - P, masked[:]))
-
             piece_max = stat_pool.tile([P, 3], F32)
-            for j, (first, piece) in enumerate(pieces):
+            for i, (first, piece) in enumerate(pieces):
                 nc.vector.tensor_reduce(
-                    out=piece_max[:, j : j + 1], in_=piece, axis=AXIS.X, op=ALU.max
+                    out=piece_max[:, i : i + 1], in_=piece, axis=AXIS.X, op=ALU.max
                 )
+            state["pieces"] = pieces
+            state["piece_max"] = piece_max
+
+        def negate_maximum(n):
+            if not 0 <= n < TILES:
+                return
+            state = tiles[n]
             minus_max = stat_pool.tile([P, 1], F32)
             nc.vector.tensor_reduce(
-                out=minus_max[:], in_=piece_max[:, : len(pieces)], axis=AXIS.X, op=ALU.max, negate=True
+                out=minus_max[:],
+                in_=state["piece_max"][:, : len(state["pieces"])],
+                axis=AXIS.X,
+                op=ALU.max,
+                negate=True,
             )
+            state["minus_max"] = minus_max
 
+        def exponentials(n):
+            if not 0 <= n < TILES:
+                return
+            state = tiles[n]
             piece_sum = stat_pool.tile([P, 3], F32)
-            for j, (first, piece) in enumerate(pieces):
+            for i, (first, piece) in enumerate(state["pieces"]):
                 nc.scalar.activation(
-                    out=e_rows[qi][:, first : first + piece.shape[1]],
+                    out=e_rows[state["qi"]][:, first : first + piece.shape[1]],
                     in_=piece,
                     func=ACT.Exp,
-                    bias=minus_max[:, 0:1],
+                    bias=state["minus_max"][:, 0:1],
                     scale=1.0,
-                    accum_out=piece_sum[:, j : j + 1],
+                    accum_out=piece_sum[:, i : i + 1],
                 )
+            state["piece_sum"] = piece_sum
+
+        def sum_pieces(n):
+            if not 0 <= n < TILES:
+                return
+            state = tiles[n]
             row_sum = stat_pool.tile([P, 1], F32)
             nc.vector.tensor_reduce(
-                out=row_sum[:], in_=piece_sum[:, : len(pieces)], axis=AXIS.X, op=ALU.add
+                out=row_sum[:],
+                in_=state["piece_sum"][:, : len(state["pieces"])],
+                axis=AXIS.X,
+                op=ALU.add,
             )
-            inv_sum = stat_pool.tile([P, 1], F32)
-            nc.vector.reciprocal(out=inv_sum[:], in_=row_sum[:])
+            state["row_sum"] = row_sum
 
-            flipped = e_psum.tile([P, 2 * (KEYS // K_PASS), P], F32)
-            e_words = e_rows[qi][:].bitcast(F32)
-            for w in range(2 * passes):
+        def invert_sum(n):
+            if not 0 <= n < TILES:
+                return
+            inv_sum = stat_pool.tile([P, 1], F32)
+            nc.vector.reciprocal(out=inv_sum[:], in_=tiles[n]["row_sum"][:])
+            tiles[n]["inv_sum"] = inv_sum
+
+        def flip_e(n):
+            if not 0 <= n < TILES:
+                return
+            e_tile = e_rows[tiles[n]["qi"]]
+            flipped = e_psum.tile([P, KEYS // (2 * P), P], F32)
+            e_words = e_tile[:].bitcast(F32)
+            for w in range(e_tile.shape[1] // (2 * P)):
                 nc.tensor.transpose(flipped[:, w, :], e_words[:, w * P : (w + 1) * P], identity[:])
-            grouped = work_pool.tile([P, KEYS // K_PASS * K_PASS], BF16, align_bytes=64)
+            tiles[n]["flipped"] = flipped
+            tiles[n]["passes"] = e_tile.shape[1] // K_PASS
+
+        def copy_e(n):
+            if not 0 <= n < TILES:
+                return
+            passes = tiles[n]["passes"]
+            grouped = work_pool.tile([P, KEYS], BF16, align_bytes=64)
             grouped_words = grouped[:].bitcast(F32).rearrange("p (g i u) -> p g i u", i=P, u=2)
             nc.scalar.copy(
                 out=grouped_words[:, :passes],
-                in_=flipped[:, : 2 * passes, :].rearrange("p (g u) i -> p g i u", u=2),
+                in_=tiles[n]["flipped"][:, : 2 * passes, :].rearrange("p (g u) i -> p g i u", u=2),
             )
-            e_codes = work_pool.tile([P, KEYS // K_PASS * P], U32, align_bytes=64)
-            e_scales = work_pool.tile([P, KEYS // K_PASS * P], U8, align_bytes=64)
+            tiles[n]["grouped"] = grouped
+
+        def quantise_e(n):
+            if not 0 <= n < TILES:
+                return
+            passes = tiles[n]["passes"]
+            e_codes = work_pool.tile([P, KEYS // PACK], U32, align_bytes=64)
+            e_scales = work_pool.tile([P, KEYS // PACK], U8, align_bytes=64)
             nc.vector.quantize_mx(
                 out=e_codes[:, : passes * P].bitcast(FP8X4),
                 scales=e_scales[:, : passes * P],
-                in_=grouped[:, : passes * K_PASS],
+                in_=tiles[n]["grouped"][:, : passes * K_PASS],
             )
+            tiles[n]["e_codes"] = e_codes
+            tiles[n]["e_scales"] = e_scales
 
+        def mix_values(n):
+            if not 0 <= n < TILES:
+                return
+            state = tiles[n]
             mixed = out_psum.tile([P, FEATURES], F32)
-            for g in range(passes):
+            for g in range(state["passes"]):
                 nc.tensor.matmul_mx(
                     out=mixed[:],
-                    lhsT=e_codes[:, g * P : (g + 1) * P].bitcast(FP8X4),
-                    lhsT_scale=e_scales[:, g * P : (g + 1) * P],
-                    rhs=batch["v_codes"][:, g * FEATURES : (g + 1) * FEATURES].bitcast(FP8X4),
-                    rhs_scale=batch["v_scales"][:, g * FEATURES : (g + 1) * FEATURES],
+                    lhsT=state["e_codes"][:, g * P : (g + 1) * P].bitcast(FP8X4),
+                    lhsT_scale=state["e_scales"][:, g * P : (g + 1) * P],
+                    rhs=state["batch"]["v_codes"][:, g * FEATURES : (g + 1) * FEATURES].bitcast(FP8X4),
+                    rhs_scale=state["batch"]["v_scales"][:, g * FEATURES : (g + 1) * FEATURES],
                     start=(g == 0),
-                    stop=(g == passes - 1),
+                    stop=(g == state["passes"] - 1),
                 )
+            state["mixed"] = mixed
+
+        def finish(n):
+            if not 0 <= n < TILES:
+                return
+            state = tiles[n]
+            qi = state["qi"]
             result = work_pool.tile([P, FEATURES], F32)
             nc.vector.scalar_tensor_tensor(
                 out=result[:],
-                in0=mixed[:],
-                scalar=inv_sum[:, 0:1],
-                in1=batch["residual"][:, qi + FIRST_QUERY // P, :],
+                in0=state["mixed"][:],
+                scalar=state["inv_sum"][:, 0:1],
+                in1=state["batch"]["residual"][:, qi + FIRST_QUERY // P, :],
                 op0=ALU.mult,
                 op1=ALU.add,
             )
-            nc.sync.dma_start(out=out[b, queries, :], in_=result[:])
+            nc.sync.dma_start(out=out[state["b"], qi * P : (qi + 1) * P, :], in_=result[:])
 
-        batch = open_batch()
-        for part in range(PARTS):
-            prepare(0, part, batch)
-        for b in range(BATCHES):
-            following = open_batch() if b + 1 < BATCHES else None
-            for qi in range(QUERY_TILES):
-                attend(b, qi, batch)
-                if following is not None and qi < PARTS:
-                    prepare(b + 1, qi, following)
-            batch = following
+        for s in range(-LOAD_AHEAD, TILES + 1):
+            for group in groups_due(s + LOAD_AHEAD):
+                load_rows(group)
+            quantise_e(s - 1)
+            score(s + 1)
+            mix_values(s - 1)
+            exponentials(s)
+            for group in groups_due(s + SQUARE_AHEAD):
+                square_sums(group)
+            for group in groups_due(s + FLIP_AHEAD):
+                normalise(group)
+            flip_e(s)
+            for group in groups_due(s + FLIP_AHEAD):
+                flip_rows(group)
+            for group in groups_due(s + QUANTISE_AHEAD):
+                quantise_rows(group)
+            for group in groups_due(s + FLIP_AHEAD):
+                quantise_values(group)
+            for group in groups_due(s + SQUARE_AHEAD):
+                regroup_values(group)
+            piece_maxima(s + 1)
+            sum_pieces(s)
+            negate_maximum(s + 1)
+            invert_sum(s)
+            finish(s - 1)
+            copy_e(s)
+            for group in groups_due(s + FLIP_AHEAD):
+                copy_rows(group)

@@ -27,9 +27,10 @@ PAIR = 2
 EPS = 1e-12
 NEG = -1e15
 
-LOAD_AHEAD = 6
-SQUARE_AHEAD = 4
-FLIP_AHEAD = 3
+LOAD_AHEAD = 7
+SQUARE_AHEAD = 5
+FLIP_AHEAD = 4
+COPY_AHEAD = 3
 QUANTISE_AHEAD = 2
 
 FLOPS = 2 * 2 * BATCHES * FEATURES * (384 * 512 + 512 * 1024)
@@ -61,7 +62,7 @@ def tile_spatialangularattention_pa_t_kernel(tc, q_rows, k_rows, v_rows, out):
         raw_pool = stack.enter_context(tc.tile_pool(name="raw", bufs=6))
         row_pool = stack.enter_context(tc.tile_pool(name="rows", bufs=4))
         value_pool = stack.enter_context(tc.tile_pool(name="values", bufs=2))
-        batch_pool = stack.enter_context(tc.tile_pool(name="batch", bufs=2))
+        batch_pool = stack.enter_context(tc.tile_pool(name="batch", bufs=3))
         stat_pool = stack.enter_context(tc.tile_pool(name="stats", bufs=4))
         work_pool = stack.enter_context(tc.tile_pool(name="work", bufs=3))
         flip_psum = stack.enter_context(tc.psum_pool(name="flip_psum", bufs=2))
@@ -85,6 +86,8 @@ def tile_spatialangularattention_pa_t_kernel(tc, q_rows, k_rows, v_rows, out):
         )
         minus_half = const.tile([P, PAIR], F32)
         nc.vector.memset(minus_half[:], -0.5)
+        minus_one = const.tile([P, 1], F32)
+        nc.vector.memset(minus_one[:], -1.0)
 
         e_rows = []
         for qi in range(QUERY_TILES):
@@ -98,6 +101,12 @@ def tile_spatialangularattention_pa_t_kernel(tc, q_rows, k_rows, v_rows, out):
         batches = {}
         groups = {}
         tiles = {}
+
+        def copy_words(sbuf_words, psum_words, whole_bank):
+            if whole_bank:
+                nc.scalar.copy(out=sbuf_words, in_=psum_words)
+            else:
+                nc.vector.tensor_copy(out=sbuf_words, in_=psum_words)
 
 
         def open_batch(b):
@@ -208,10 +217,8 @@ def tile_spatialangularattention_pa_t_kernel(tc, q_rows, k_rows, v_rows, out):
             count = state["count"]
             grouped = row_pool.tile([P, PAIR * FEATURES], BF16, align_bytes=64)
             grouped_words = grouped[:].bitcast(F32).rearrange("p (t r u) -> p t r u", t=PAIR, u=2)
-            nc.scalar.copy(
-                out=grouped_words[:, :count],
-                in_=state["flipped"][:, :count].rearrange("p t u r -> p t r u"),
-            )
+            flipped_words = state["flipped"][:, :count].rearrange("p t u r -> p t r u")
+            copy_words(grouped_words[:, :count], flipped_words, count == PAIR)
             state["grouped"] = grouped
 
         def quantise_rows(group):
@@ -325,25 +332,24 @@ def tile_spatialangularattention_pa_t_kernel(tc, q_rows, k_rows, v_rows, out):
                 )
             state["piece_sum"] = piece_sum
 
-        def sum_pieces(n):
-            if not 0 <= n < TILES:
-                return
-            state = tiles[n]
-            row_sum = stat_pool.tile([P, 1], F32)
-            nc.vector.tensor_reduce(
-                out=row_sum[:],
-                in_=state["piece_sum"][:, : len(state["pieces"])],
-                axis=AXIS.X,
-                op=ALU.add,
-            )
-            state["row_sum"] = row_sum
-
         def invert_sum(n):
             if not 0 <= n < TILES:
                 return
+            state = tiles[n]
+            piece_sum = state["piece_sum"]
+            row_sum = stat_pool.tile([P, 1], F32)
+            nc.gpsimd.tensor_tensor(
+                out=row_sum[:], in0=piece_sum[:, 0:1], in1=piece_sum[:, 1:2], op=ALU.add
+            )
+            for i in range(2, len(state["pieces"])):
+                nc.gpsimd.tensor_tensor(
+                    out=row_sum[:], in0=row_sum[:], in1=piece_sum[:, i : i + 1], op=ALU.add
+                )
             inv_sum = stat_pool.tile([P, 1], F32)
-            nc.vector.reciprocal(out=inv_sum[:], in_=tiles[n]["row_sum"][:])
-            tiles[n]["inv_sum"] = inv_sum
+            nc.gpsimd.tensor_tensor(
+                out=inv_sum[:], in0=row_sum[:], in1=minus_one[:], op=ALU.pow
+            )
+            state["inv_sum"] = inv_sum
 
         def flip_e(n):
             if not 0 <= n < TILES:
@@ -362,10 +368,10 @@ def tile_spatialangularattention_pa_t_kernel(tc, q_rows, k_rows, v_rows, out):
             passes = tiles[n]["passes"]
             grouped = work_pool.tile([P, KEYS], BF16, align_bytes=64)
             grouped_words = grouped[:].bitcast(F32).rearrange("p (g i u) -> p g i u", i=P, u=2)
-            nc.scalar.copy(
-                out=grouped_words[:, :passes],
-                in_=tiles[n]["flipped"][:, : 2 * passes, :].rearrange("p (g u) i -> p g i u", u=2),
+            flipped_words = tiles[n]["flipped"][:, : 2 * passes, :].rearrange(
+                "p (g u) i -> p g i u", u=2
             )
+            copy_words(grouped_words[:, :passes], flipped_words, passes * K_PASS == KEYS)
             tiles[n]["grouped"] = grouped
 
         def quantise_e(n):
@@ -415,31 +421,30 @@ def tile_spatialangularattention_pa_t_kernel(tc, q_rows, k_rows, v_rows, out):
             )
             nc.sync.dma_start(out=out[state["b"], qi * P : (qi + 1) * P, :], in_=result[:])
 
-        for s in range(-LOAD_AHEAD, TILES + 1):
+        for s in range(-LOAD_AHEAD, TILES + 3):
             for group in groups_due(s + LOAD_AHEAD):
                 load_rows(group)
-            quantise_e(s - 1)
             score(s + 1)
-            mix_values(s - 1)
-            exponentials(s)
+            mix_values(s - 3)
             for group in groups_due(s + SQUARE_AHEAD):
                 square_sums(group)
+            copy_e(s - 2)
+            for group in groups_due(s + COPY_AHEAD):
+                copy_rows(group)
+            exponentials(s)
             for group in groups_due(s + FLIP_AHEAD):
                 normalise(group)
-            flip_e(s)
-            for group in groups_due(s + FLIP_AHEAD):
-                flip_rows(group)
             for group in groups_due(s + QUANTISE_AHEAD):
                 quantise_rows(group)
             for group in groups_due(s + FLIP_AHEAD):
                 quantise_values(group)
             for group in groups_due(s + SQUARE_AHEAD):
                 regroup_values(group)
+            quantise_e(s - 2)
             piece_maxima(s + 1)
-            sum_pieces(s)
+            finish(s - 3)
             negate_maximum(s + 1)
-            invert_sum(s)
-            finish(s - 1)
-            copy_e(s)
+            invert_sum(s - 1)
+            flip_e(s - 1)
             for group in groups_due(s + FLIP_AHEAD):
-                copy_rows(group)
+                flip_rows(group)

@@ -86,8 +86,6 @@ def tile_spatialangularattention_pa_t_kernel(tc, q_rows, k_rows, v_rows, out):
         )
         minus_half = const.tile([P, PAIR], F32)
         nc.vector.memset(minus_half[:], -0.5)
-        minus_one = const.tile([P, 1], F32)
-        nc.vector.memset(minus_one[:], -1.0)
 
         e_rows = []
         for qi in range(QUERY_TILES):
@@ -101,12 +99,6 @@ def tile_spatialangularattention_pa_t_kernel(tc, q_rows, k_rows, v_rows, out):
         batches = {}
         groups = {}
         tiles = {}
-
-        def copy_words(sbuf_words, psum_words, whole_bank):
-            if whole_bank:
-                nc.scalar.copy(out=sbuf_words, in_=psum_words)
-            else:
-                nc.vector.tensor_copy(out=sbuf_words, in_=psum_words)
 
 
         def open_batch(b):
@@ -217,8 +209,10 @@ def tile_spatialangularattention_pa_t_kernel(tc, q_rows, k_rows, v_rows, out):
             count = state["count"]
             grouped = row_pool.tile([P, PAIR * FEATURES], BF16, align_bytes=64)
             grouped_words = grouped[:].bitcast(F32).rearrange("p (t r u) -> p t r u", t=PAIR, u=2)
-            flipped_words = state["flipped"][:, :count].rearrange("p t u r -> p t r u")
-            copy_words(grouped_words[:, :count], flipped_words, count == PAIR)
+            nc.scalar.copy(
+                out=grouped_words[:, :count],
+                in_=state["flipped"][:, :count].rearrange("p t u r -> p t r u"),
+            )
             state["grouped"] = grouped
 
         def quantise_rows(group):
@@ -332,24 +326,25 @@ def tile_spatialangularattention_pa_t_kernel(tc, q_rows, k_rows, v_rows, out):
                 )
             state["piece_sum"] = piece_sum
 
-        def invert_sum(n):
+        def sum_pieces(n):
             if not 0 <= n < TILES:
                 return
             state = tiles[n]
-            piece_sum = state["piece_sum"]
             row_sum = stat_pool.tile([P, 1], F32)
-            nc.gpsimd.tensor_tensor(
-                out=row_sum[:], in0=piece_sum[:, 0:1], in1=piece_sum[:, 1:2], op=ALU.add
+            nc.vector.tensor_reduce(
+                out=row_sum[:],
+                in_=state["piece_sum"][:, : len(state["pieces"])],
+                axis=AXIS.X,
+                op=ALU.add,
             )
-            for i in range(2, len(state["pieces"])):
-                nc.gpsimd.tensor_tensor(
-                    out=row_sum[:], in0=row_sum[:], in1=piece_sum[:, i : i + 1], op=ALU.add
-                )
+            state["row_sum"] = row_sum
+
+        def invert_sum(n):
+            if not 0 <= n < TILES:
+                return
             inv_sum = stat_pool.tile([P, 1], F32)
-            nc.gpsimd.tensor_tensor(
-                out=inv_sum[:], in0=row_sum[:], in1=minus_one[:], op=ALU.pow
-            )
-            state["inv_sum"] = inv_sum
+            nc.vector.reciprocal(out=inv_sum[:], in_=tiles[n]["row_sum"][:])
+            tiles[n]["inv_sum"] = inv_sum
 
         def flip_e(n):
             if not 0 <= n < TILES:
@@ -368,10 +363,10 @@ def tile_spatialangularattention_pa_t_kernel(tc, q_rows, k_rows, v_rows, out):
             passes = tiles[n]["passes"]
             grouped = work_pool.tile([P, KEYS], BF16, align_bytes=64)
             grouped_words = grouped[:].bitcast(F32).rearrange("p (g i u) -> p g i u", i=P, u=2)
-            flipped_words = tiles[n]["flipped"][:, : 2 * passes, :].rearrange(
-                "p (g u) i -> p g i u", u=2
+            nc.scalar.copy(
+                out=grouped_words[:, :passes],
+                in_=tiles[n]["flipped"][:, : 2 * passes, :].rearrange("p (g u) i -> p g i u", u=2),
             )
-            copy_words(grouped_words[:, :passes], flipped_words, passes * K_PASS == KEYS)
             tiles[n]["grouped"] = grouped
 
         def quantise_e(n):
@@ -442,9 +437,10 @@ def tile_spatialangularattention_pa_t_kernel(tc, q_rows, k_rows, v_rows, out):
                 regroup_values(group)
             quantise_e(s - 2)
             piece_maxima(s + 1)
-            finish(s - 3)
+            sum_pieces(s - 1)
             negate_maximum(s + 1)
             invert_sum(s - 1)
+            finish(s - 3)
             flip_e(s - 1)
             for group in groups_due(s + FLIP_AHEAD):
                 flip_rows(group)

@@ -27,8 +27,8 @@ PAIR = 2
 EPS = 1e-12
 NEG = -1e15
 
-LOAD_AHEAD = 7
-SQUARE_AHEAD = 5
+LOAD_AHEAD = 8
+SQUARE_AHEAD = 6
 FLIP_AHEAD = 4
 COPY_AHEAD = 3
 QUANTISE_AHEAD = 2
@@ -59,8 +59,8 @@ def tile_spatialangularattention_pa_t_kernel(tc, q_rows, k_rows, v_rows, out):
     nc = tc.nc
     with ExitStack() as stack:
         const = stack.enter_context(tc.tile_pool(name="const", bufs=1))
-        raw_pool = stack.enter_context(tc.tile_pool(name="raw", bufs=6))
-        row_pool = stack.enter_context(tc.tile_pool(name="rows", bufs=4))
+        raw_pool = stack.enter_context(tc.tile_pool(name="raw", bufs=8))
+        row_pool = stack.enter_context(tc.tile_pool(name="rows", bufs=6))
         value_pool = stack.enter_context(tc.tile_pool(name="values", bufs=2))
         batch_pool = stack.enter_context(tc.tile_pool(name="batch", bufs=3))
         stat_pool = stack.enter_context(tc.tile_pool(name="stats", bufs=4))
@@ -84,7 +84,7 @@ def tile_spatialangularattention_pa_t_kernel(tc, q_rows, k_rows, v_rows, out):
             base=0,
             channel_multiplier=1,
         )
-        minus_half = const.tile([P, PAIR], F32)
+        minus_half = const.tile([P, 2 * PAIR], F32)
         nc.vector.memset(minus_half[:], -0.5)
 
         e_rows = []
@@ -98,6 +98,7 @@ def tile_spatialangularattention_pa_t_kernel(tc, q_rows, k_rows, v_rows, out):
 
         batches = {}
         groups = {}
+        norms = {}
         tiles = {}
 
 
@@ -159,38 +160,49 @@ def tile_spatialangularattention_pa_t_kernel(tc, q_rows, k_rows, v_rows, out):
             )
 
         def square_sums(group):
+            b, j = group
             state = groups[group]
             count = state["count"]
+            if j % 2 == 0:
+                square_sum = stat_pool.tile([P, 2 * PAIR], F32)
+                norms[(b, j // 2)] = {"square_sum": square_sum}
+            shared = norms[(b, j // 2)]
             unit = row_pool.tile([P, PAIR, FEATURES], BF16)
-            square_sum = stat_pool.tile([P, PAIR], F32)
             for t in range(count):
+                column = PAIR * (j % 2) + t
                 nc.scalar.activation(
                     out=unit[:, t, :],
                     in_=state["raw"][:, t, :],
                     func=ACT.Square,
-                    accum_out=square_sum[:, t : t + 1],
+                    accum_out=shared["square_sum"][:, column : column + 1],
                 )
-            floored = stat_pool.tile([P, PAIR], F32)
-            nc.gpsimd.tensor_scalar_max(
-                out=floored[:, :count], in0=square_sum[:, :count], scalar1=EPS * EPS
-            )
-            inv_norm = stat_pool.tile([P, PAIR], F32)
-            nc.gpsimd.tensor_tensor(
-                out=inv_norm[:, :count],
-                in0=floored[:, :count],
-                in1=minus_half[:, :count],
-                op=ALU.pow,
-            )
             state["unit"] = unit
-            state["inv_norm"] = inv_norm
+            if j % 2 == 1:
+                columns = PAIR + count
+                floored = stat_pool.tile([P, 2 * PAIR], F32)
+                nc.gpsimd.tensor_scalar_max(
+                    out=floored[:, :columns],
+                    in0=shared["square_sum"][:, :columns],
+                    scalar1=EPS * EPS,
+                )
+                inv_norm = stat_pool.tile([P, 2 * PAIR], F32)
+                nc.gpsimd.tensor_tensor(
+                    out=inv_norm[:, :columns],
+                    in0=floored[:, :columns],
+                    in1=minus_half[:, :columns],
+                    op=ALU.pow,
+                )
+                shared["inv_norm"] = inv_norm
 
         def normalise(group):
+            b, j = group
             state = groups[group]
             for t in range(state["count"]):
+                column = PAIR * (j % 2) + t
                 nc.vector.tensor_scalar_mul(
                     out=state["unit"][:, t, :],
                     in0=state["raw"][:, t, :],
-                    scalar1=state["inv_norm"][:, t : t + 1],
+                    scalar1=norms[(b, j // 2)]["inv_norm"][:, column : column + 1],
                 )
 
         def flip_rows(group):
@@ -330,12 +342,14 @@ def tile_spatialangularattention_pa_t_kernel(tc, q_rows, k_rows, v_rows, out):
             if not 0 <= n < TILES:
                 return
             state = tiles[n]
+            count = len(state["pieces"])
+            copied = stat_pool.tile([P, 3], F32)
             row_sum = stat_pool.tile([P, 1], F32)
-            nc.vector.tensor_reduce(
-                out=row_sum[:],
-                in_=state["piece_sum"][:, : len(state["pieces"])],
-                axis=AXIS.X,
-                op=ALU.add,
+            nc.scalar.activation(
+                out=copied[:, :count],
+                in_=state["piece_sum"][:, :count],
+                func=ACT.Copy,
+                accum_out=row_sum[:],
             )
             state["row_sum"] = row_sum
 
@@ -423,6 +437,7 @@ def tile_spatialangularattention_pa_t_kernel(tc, q_rows, k_rows, v_rows, out):
             mix_values(s - 3)
             for group in groups_due(s + SQUARE_AHEAD):
                 square_sums(group)
+            sum_pieces(s - 1)
             copy_e(s - 2)
             for group in groups_due(s + COPY_AHEAD):
                 copy_rows(group)
@@ -437,10 +452,9 @@ def tile_spatialangularattention_pa_t_kernel(tc, q_rows, k_rows, v_rows, out):
                 regroup_values(group)
             quantise_e(s - 2)
             piece_maxima(s + 1)
-            sum_pieces(s - 1)
+            finish(s - 3)
             negate_maximum(s + 1)
             invert_sum(s - 1)
-            finish(s - 3)
             flip_e(s - 1)
             for group in groups_due(s + FLIP_AHEAD):
                 flip_rows(group)

@@ -286,10 +286,10 @@ def tile_spatialangularattention_pa_t_kernel(tc, q_rows, k_rows, v_rows, out):
                 return
             state = tiles[n]
             seen = state["seen"]
-            masked = work_pool.tile([P, P], F32)
+            masked = work_pool.tile([P, P + 2], F32)
             diagonal = (seen - P) % BANK
             nc.vector.tensor_tensor(
-                out=masked[:],
+                out=masked[:, :P],
                 in0=state["banks"][-1][:, diagonal : diagonal + P],
                 in1=causal[:],
                 op=ALU.add,
@@ -299,14 +299,13 @@ def tile_spatialangularattention_pa_t_kernel(tc, q_rows, k_rows, v_rows, out):
                 open_keys = min(seen - P - g * BANK, BANK)
                 if open_keys > 0:
                     pieces.append((g * BANK, bank[:, :open_keys]))
-            pieces.append((seen - P, masked[:]))
-            piece_max = stat_pool.tile([P, 3], F32)
             for i, (first, piece) in enumerate(pieces):
                 nc.vector.tensor_reduce(
-                    out=piece_max[:, i : i + 1], in_=piece, axis=AXIS.X, op=ALU.max
+                    out=masked[:, P + i : P + i + 1], in_=piece, axis=AXIS.X, op=ALU.max
                 )
+            state["masked"] = masked[:, : P + len(pieces)]
+            pieces.append((seen - P, masked[:, :P]))
             state["pieces"] = pieces
-            state["piece_max"] = piece_max
 
         def negate_maximum(n):
             if not 0 <= n < TILES:
@@ -315,7 +314,7 @@ def tile_spatialangularattention_pa_t_kernel(tc, q_rows, k_rows, v_rows, out):
             minus_max = stat_pool.tile([P, 1], F32)
             nc.vector.tensor_reduce(
                 out=minus_max[:],
-                in_=state["piece_max"][:, : len(state["pieces"])],
+                in_=state["masked"],
                 axis=AXIS.X,
                 op=ALU.max,
                 negate=True,

@@ -27,11 +27,17 @@ PAIR = 2
 EPS = 1e-12
 NEG = -1e15
 
-LOAD_AHEAD = 8
-SQUARE_AHEAD = 6
+LOAD_AHEAD = 10
+SQUARE_AHEAD = 8
 FLIP_AHEAD = 4
 COPY_AHEAD = 3
 QUANTISE_AHEAD = 2
+VALUES_LOAD_AHEAD = (8, 13)
+VALUES_REGROUP_AHEAD = (6, 11)
+VALUES_QUANTISE_AHEAD = (4, 9)
+RESIDUAL_LOAD_AHEAD = 8
+DRAIN_TILES = 3
+VECTOR_SQUARES = (0, 1)
 
 FLOPS = 2 * 2 * BATCHES * FEATURES * (384 * 512 + 512 * 1024)
 
@@ -55,14 +61,23 @@ def groups_due(n):
     return [(b, qi + 1)]
 
 
+def groups_at(s, ahead):
+    first, later = ahead
+    return [g for g in groups_due(s + first) if g[0] == 0] + [
+        g for g in groups_due(s + later) if g[0] > 0
+    ]
+
+
 def tile_spatialangularattention_pa_t_kernel(tc, q_rows, k_rows, v_rows, out):
     nc = tc.nc
     with ExitStack() as stack:
         const = stack.enter_context(tc.tile_pool(name="const", bufs=1))
-        raw_pool = stack.enter_context(tc.tile_pool(name="raw", bufs=8))
+        raw_pool = stack.enter_context(tc.tile_pool(name="raw", bufs=12))
+        junk_pool = stack.enter_context(tc.tile_pool(name="junk", bufs=2))
         row_pool = stack.enter_context(tc.tile_pool(name="rows", bufs=6))
         value_pool = stack.enter_context(tc.tile_pool(name="values", bufs=2))
         batch_pool = stack.enter_context(tc.tile_pool(name="batch", bufs=3))
+        value_code_pool = stack.enter_context(tc.tile_pool(name="value_codes", bufs=4))
         stat_pool = stack.enter_context(tc.tile_pool(name="stats", bufs=4))
         work_pool = stack.enter_context(tc.tile_pool(name="work", bufs=3))
         flip_psum = stack.enter_context(tc.psum_pool(name="flip_psum", bufs=2))
@@ -97,6 +112,7 @@ def tile_spatialangularattention_pa_t_kernel(tc, q_rows, k_rows, v_rows, out):
             e_rows.append(e_tile)
 
         batches = {}
+        values = {}
         groups = {}
         norms = {}
         tiles = {}
@@ -107,16 +123,12 @@ def tile_spatialangularattention_pa_t_kernel(tc, q_rows, k_rows, v_rows, out):
             q_scales = batch_pool.tile([P, QUERIES], U8, align_bytes=64)
             k_codes = batch_pool.tile([P, KEYS], U32, align_bytes=64)
             k_scales = batch_pool.tile([P, KEYS], U8, align_bytes=64)
-            v_codes = batch_pool.tile([P, 2 * FEATURES], U32, align_bytes=64)
-            v_scales = batch_pool.tile([P, 2 * FEATURES], U8, align_bytes=64)
             residual = batch_pool.tile([P, KEYS // P, FEATURES], BF16)
             batches[b] = {
                 "q_codes": q_codes,
                 "q_scales": q_scales,
                 "k_codes": k_codes,
                 "k_scales": k_scales,
-                "v_codes": v_codes,
-                "v_scales": v_scales,
                 "residual": residual,
             }
 
@@ -138,19 +150,30 @@ def tile_spatialangularattention_pa_t_kernel(tc, q_rows, k_rows, v_rows, out):
                 "codes": batches[b][kind + "_codes"][:, rows],
                 "scales": batches[b][kind + "_scales"][:, rows],
             }
-            if j % 4 == 1:
-                load_values(group)
 
         def load_values(group):
             b, j = group
+            if j % 4 != 1:
+                return
             g = j // 4
             first = g * K_PASS
+            if g == 0:
+                v_codes = value_code_pool.tile([P, 2 * FEATURES], U32, align_bytes=64)
+                v_scales = value_code_pool.tile([P, 2 * FEATURES], U8, align_bytes=64)
+                values[b] = {"codes": v_codes, "scales": v_scales}
             raw_values = value_pool.tile([P, PACK, FEATURES], BF16)
             nc.sync.dma_start(
                 out=raw_values[:].rearrange("p (u e) d -> p u e d", e=2),
                 in_=v_rows[b, first : first + K_PASS, :].rearrange("(u p e) d -> p u e d", p=P, e=2),
             )
-            groups[group]["raw_values"] = raw_values
+            values[b][g] = {"raw": raw_values}
+
+        def load_residual(group):
+            b, j = group
+            if j % 4 != 1:
+                return
+            g = j // 4
+            first = g * K_PASS
             skip = max(FIRST_QUERY - first, 0) // P
             nc.sync.dma_start(
                 out=batches[b]["residual"][:, g * PACK + skip : (g + 1) * PACK, :],
@@ -167,16 +190,27 @@ def tile_spatialangularattention_pa_t_kernel(tc, q_rows, k_rows, v_rows, out):
                 square_sum = stat_pool.tile([P, 2 * PAIR], F32)
                 norms[(b, j // 2)] = {"square_sum": square_sum}
             shared = norms[(b, j // 2)]
-            unit = row_pool.tile([P, PAIR, FEATURES], BF16)
             for t in range(count):
                 column = PAIR * (j % 2) + t
-                nc.scalar.activation(
-                    out=unit[:, t, :],
-                    in_=state["raw"][:, t, :],
-                    func=ACT.Square,
-                    accum_out=shared["square_sum"][:, column : column + 1],
-                )
-            state["unit"] = unit
+                if group == VECTOR_SQUARES:
+                    vector_squares = junk_pool.tile([P, FEATURES], F32)
+                    nc.vector.scalar_tensor_tensor(
+                        out=vector_squares[:],
+                        in0=state["raw"][:, t, :],
+                        scalar=1.0,
+                        in1=state["raw"][:, t, :],
+                        op0=ALU.mult,
+                        op1=ALU.mult,
+                        accum_out=shared["square_sum"][:, column : column + 1],
+                    )
+                else:
+                    squares = junk_pool.tile([P, FEATURES], BF16)
+                    nc.scalar.activation(
+                        out=squares[:],
+                        in_=state["raw"][:, t, :],
+                        func=ACT.Square,
+                        accum_out=shared["square_sum"][:, column : column + 1],
+                    )
             if j % 2 == 1:
                 columns = PAIR + count
                 floored = stat_pool.tile([P, 2 * PAIR], F32)
@@ -197,10 +231,12 @@ def tile_spatialangularattention_pa_t_kernel(tc, q_rows, k_rows, v_rows, out):
         def normalise(group):
             b, j = group
             state = groups[group]
+            unit = row_pool.tile([P, PAIR, FEATURES], BF16)
+            state["unit"] = unit
             for t in range(state["count"]):
                 column = PAIR * (j % 2) + t
                 nc.vector.tensor_scalar_mul(
-                    out=state["unit"][:, t, :],
+                    out=unit[:, t, :],
                     in0=state["raw"][:, t, :],
                     scalar1=norms[(b, j // 2)]["inv_norm"][:, column : column + 1],
                 )
@@ -236,24 +272,25 @@ def tile_spatialangularattention_pa_t_kernel(tc, q_rows, k_rows, v_rows, out):
             )
 
         def regroup_values(group):
-            if "raw_values" not in groups[group]:
+            b, j = group
+            if j % 4 != 1:
                 return
             grouped_values = value_pool.tile([P, FEATURES, PACK], BF16, align_bytes=64)
             nc.vector.tensor_copy(
                 out=grouped_values[:].rearrange("p (c i) s -> p c s i", i=4),
-                in_=groups[group]["raw_values"][:].rearrange("p s (c i) -> p c s i", i=4),
+                in_=values[b][j // 4]["raw"][:].rearrange("p s (c i) -> p c s i", i=4),
             )
-            groups[group]["grouped_values"] = grouped_values
+            values[b][j // 4]["grouped"] = grouped_values
 
         def quantise_values(group):
-            if "raw_values" not in groups[group]:
-                return
             b, j = group
+            if j % 4 != 1:
+                return
             columns = slice((j // 4) * FEATURES, (j // 4 + 1) * FEATURES)
             nc.vector.quantize_mx(
-                out=batches[b]["v_codes"][:, columns].bitcast(FP8X4),
-                scales=batches[b]["v_scales"][:, columns],
-                in_=groups[group]["grouped_values"][:].rearrange("p d s -> p (d s)"),
+                out=values[b]["codes"][:, columns].bitcast(FP8X4),
+                scales=values[b]["scales"][:, columns],
+                in_=values[b][j // 4]["grouped"][:].rearrange("p d s -> p (d s)"),
             )
 
 
@@ -400,14 +437,18 @@ def tile_spatialangularattention_pa_t_kernel(tc, q_rows, k_rows, v_rows, out):
             if not 0 <= n < TILES:
                 return
             state = tiles[n]
-            mixed = out_psum.tile([P, FEATURES], F32)
+            if n < TILES - DRAIN_TILES:
+                mixed = out_psum.tile([P, FEATURES], F32)
+            else:
+                bank = score_psum.tile([P, BANK], F32)
+                mixed = bank
             for g in range(state["passes"]):
                 nc.tensor.matmul_mx(
                     out=mixed[:],
                     lhsT=state["e_codes"][:, g * P : (g + 1) * P].bitcast(FP8X4),
                     lhsT_scale=state["e_scales"][:, g * P : (g + 1) * P],
-                    rhs=state["batch"]["v_codes"][:, g * FEATURES : (g + 1) * FEATURES].bitcast(FP8X4),
-                    rhs_scale=state["batch"]["v_scales"][:, g * FEATURES : (g + 1) * FEATURES],
+                    rhs=values[state["b"]]["codes"][:, g * FEATURES : (g + 1) * FEATURES].bitcast(FP8X4),
+                    rhs_scale=values[state["b"]]["scales"][:, g * FEATURES : (g + 1) * FEATURES],
                     start=(g == 0),
                     stop=(g == state["passes"] - 1),
                 )
@@ -432,6 +473,12 @@ def tile_spatialangularattention_pa_t_kernel(tc, q_rows, k_rows, v_rows, out):
         for s in range(-LOAD_AHEAD, TILES + 3):
             for group in groups_due(s + LOAD_AHEAD):
                 load_rows(group)
+            for group in groups_at(s, VALUES_LOAD_AHEAD):
+                load_values(group)
+            for group in groups_due(s + RESIDUAL_LOAD_AHEAD):
+                load_residual(group)
+            if s >= TILES:
+                flip_e(s - 1)
             score(s + 1)
             mix_values(s - 3)
             for group in groups_due(s + SQUARE_AHEAD):
@@ -445,15 +492,16 @@ def tile_spatialangularattention_pa_t_kernel(tc, q_rows, k_rows, v_rows, out):
                 normalise(group)
             for group in groups_due(s + QUANTISE_AHEAD):
                 quantise_rows(group)
-            for group in groups_due(s + FLIP_AHEAD):
+            for group in groups_at(s, VALUES_QUANTISE_AHEAD):
                 quantise_values(group)
-            for group in groups_due(s + SQUARE_AHEAD):
+            for group in groups_at(s, VALUES_REGROUP_AHEAD):
                 regroup_values(group)
             quantise_e(s - 2)
             piece_maxima(s + 1)
             finish(s - 3)
             negate_maximum(s + 1)
             invert_sum(s - 1)
-            flip_e(s - 1)
+            if s < TILES:
+                flip_e(s - 1)
             for group in groups_due(s + FLIP_AHEAD):
                 flip_rows(group)

@@ -38,6 +38,7 @@ VALUES_QUANTISE_AHEAD = (4, 9)
 RESIDUAL_LOAD_AHEAD = 8
 DRAIN_TILES = 3
 VECTOR_SQUARES = (0, 1)
+VECTOR_COPY_GROUP = 3
 
 FLOPS = 2 * 2 * BATCHES * FEATURES * (384 * 512 + 512 * 1024)
 
@@ -78,11 +79,10 @@ def tile_spatialangularattention_pa_t_kernel(tc, q_rows, k_rows, v_rows, out):
         value_pool = stack.enter_context(tc.tile_pool(name="values", bufs=2))
         batch_pool = stack.enter_context(tc.tile_pool(name="batch", bufs=3))
         value_code_pool = stack.enter_context(tc.tile_pool(name="value_codes", bufs=4))
-        stat_pool = stack.enter_context(tc.tile_pool(name="stats", bufs=4))
-        work_pool = stack.enter_context(tc.tile_pool(name="work", bufs=3))
-        flip_psum = stack.enter_context(tc.psum_pool(name="flip_psum", bufs=2))
+        stat_pool = stack.enter_context(tc.tile_pool(name="stats", bufs=6))
+        work_pool = stack.enter_context(tc.tile_pool(name="work", bufs=4))
+        flip_psum = stack.enter_context(tc.psum_pool(name="flip_psum", bufs=3))
         score_psum = stack.enter_context(tc.psum_pool(name="score_psum", bufs=4))
-        e_psum = stack.enter_context(tc.psum_pool(name="e_psum", bufs=1))
         out_psum = stack.enter_context(tc.psum_pool(name="out_psum", bufs=1))
         stack.enter_context(tc.manual_schedule())
 
@@ -257,7 +257,8 @@ def tile_spatialangularattention_pa_t_kernel(tc, q_rows, k_rows, v_rows, out):
             count = state["count"]
             grouped = row_pool.tile([P, PAIR * FEATURES], BF16, align_bytes=64)
             grouped_words = grouped[:].bitcast(F32).rearrange("p (t r u) -> p t r u", t=PAIR, u=2)
-            nc.scalar.copy(
+            copy = nc.vector.tensor_copy if group[1] == VECTOR_COPY_GROUP else nc.scalar.copy
+            copy(
                 out=grouped_words[:, :count],
                 in_=state["flipped"][:, :count].rearrange("p t u r -> p t r u"),
             )
@@ -400,7 +401,7 @@ def tile_spatialangularattention_pa_t_kernel(tc, q_rows, k_rows, v_rows, out):
             if not 0 <= n < TILES:
                 return
             e_tile = e_rows[tiles[n]["qi"]]
-            flipped = e_psum.tile([P, KEYS // (2 * P), P], F32)
+            flipped = flip_psum.tile([P, KEYS // (2 * P), P], F32)
             e_words = e_tile[:].bitcast(F32)
             for w in range(e_tile.shape[1] // (2 * P)):
                 nc.tensor.transpose(flipped[:, w, :], e_words[:, w * P : (w + 1) * P], identity[:])
@@ -470,7 +471,7 @@ def tile_spatialangularattention_pa_t_kernel(tc, q_rows, k_rows, v_rows, out):
             )
             nc.sync.dma_start(out=out[state["b"], qi * P : (qi + 1) * P, :], in_=result[:])
 
-        for s in range(-LOAD_AHEAD, TILES + 3):
+        for s in range(-LOAD_AHEAD, TILES + 4):
             for group in groups_due(s + LOAD_AHEAD):
                 load_rows(group)
             for group in groups_at(s, VALUES_LOAD_AHEAD):
@@ -480,7 +481,7 @@ def tile_spatialangularattention_pa_t_kernel(tc, q_rows, k_rows, v_rows, out):
             if s >= TILES:
                 flip_e(s - 1)
             score(s + 1)
-            mix_values(s - 3)
+            mix_values(s - 4)
             for group in groups_due(s + SQUARE_AHEAD):
                 square_sums(group)
             sum_pieces(s - 1)
@@ -496,9 +497,9 @@ def tile_spatialangularattention_pa_t_kernel(tc, q_rows, k_rows, v_rows, out):
                 quantise_values(group)
             for group in groups_at(s, VALUES_REGROUP_AHEAD):
                 regroup_values(group)
-            quantise_e(s - 2)
+            quantise_e(s - 3)
             piece_maxima(s + 1)
-            finish(s - 3)
+            finish(s - 4)
             negate_maximum(s + 1)
             invert_sum(s - 1)
             if s < TILES:

@@ -75,7 +75,7 @@ def tile_spatialangularattention_pa_t_kernel(tc, q_rows, k_rows, v_rows, out):
         const = stack.enter_context(tc.tile_pool(name="const", bufs=1))
         raw_pool = stack.enter_context(tc.tile_pool(name="raw", bufs=12))
         junk_pool = stack.enter_context(tc.tile_pool(name="junk", bufs=2))
-        row_pool = stack.enter_context(tc.tile_pool(name="rows", bufs=6))
+        row_pool = stack.enter_context(tc.tile_pool(name="rows", bufs=9))
         value_pool = stack.enter_context(tc.tile_pool(name="values", bufs=2))
         batch_pool = stack.enter_context(tc.tile_pool(name="batch", bufs=3))
         value_code_pool = stack.enter_context(tc.tile_pool(name="value_codes", bufs=4))
@@ -190,6 +190,8 @@ def tile_spatialangularattention_pa_t_kernel(tc, q_rows, k_rows, v_rows, out):
                 square_sum = stat_pool.tile([P, 2 * PAIR], F32)
                 norms[(b, j // 2)] = {"square_sum": square_sum}
             shared = norms[(b, j // 2)]
+            unit = row_pool.tile([P, PAIR, FEATURES], BF16)
+            state["unit"] = unit
             for t in range(count):
                 column = PAIR * (j % 2) + t
                 if group == VECTOR_SQUARES:
@@ -204,9 +206,8 @@ def tile_spatialangularattention_pa_t_kernel(tc, q_rows, k_rows, v_rows, out):
                         accum_out=shared["square_sum"][:, column : column + 1],
                     )
                 else:
-                    squares = junk_pool.tile([P, FEATURES], BF16)
                     nc.scalar.activation(
-                        out=squares[:],
+                        out=unit[:, t, :],
                         in_=state["raw"][:, t, :],
                         func=ACT.Square,
                         accum_out=shared["square_sum"][:, column : column + 1],
@@ -231,12 +232,10 @@ def tile_spatialangularattention_pa_t_kernel(tc, q_rows, k_rows, v_rows, out):
         def normalise(group):
             b, j = group
             state = groups[group]
-            unit = row_pool.tile([P, PAIR, FEATURES], BF16)
-            state["unit"] = unit
             for t in range(state["count"]):
                 column = PAIR * (j % 2) + t
                 nc.vector.tensor_scalar_mul(
-                    out=unit[:, t, :],
+                    out=state["unit"][:, t, :],
                     in0=state["raw"][:, t, :],
                     scalar1=norms[(b, j // 2)]["inv_norm"][:, column : column + 1],
                 )
@@ -257,7 +256,8 @@ def tile_spatialangularattention_pa_t_kernel(tc, q_rows, k_rows, v_rows, out):
             count = state["count"]
             grouped = row_pool.tile([P, PAIR * FEATURES], BF16, align_bytes=64)
             grouped_words = grouped[:].bitcast(F32).rearrange("p (t r u) -> p t r u", t=PAIR, u=2)
-            copy = nc.vector.tensor_copy if group[1] == VECTOR_COPY_GROUP else nc.scalar.copy
+            by_vector = group[1] == VECTOR_COPY_GROUP and group[0] < BATCHES - 1
+            copy = nc.vector.tensor_copy if by_vector else nc.scalar.copy
             copy(
                 out=grouped_words[:, :count],
                 in_=state["flipped"][:, :count].rearrange("p t u r -> p t r u"),

@@ -38,7 +38,7 @@ VALUES_QUANTISE_AHEAD = (4, 9)
 RESIDUAL_LOAD_AHEAD = 8
 DRAIN_TILES = 3
 VECTOR_SQUARES = (0, 1)
-VECTOR_COPY_GROUP = 3
+VECTOR_COPY_GROUPS = (3, 7)
 
 FLOPS = 2 * 2 * BATCHES * FEATURES * (384 * 512 + 512 * 1024)
 
@@ -256,7 +256,7 @@ def tile_spatialangularattention_pa_t_kernel(tc, q_rows, k_rows, v_rows, out):
             count = state["count"]
             grouped = row_pool.tile([P, PAIR * FEATURES], BF16, align_bytes=64)
             grouped_words = grouped[:].bitcast(F32).rearrange("p (t r u) -> p t r u", t=PAIR, u=2)
-            by_vector = group[1] == VECTOR_COPY_GROUP and group[0] < BATCHES - 1
+            by_vector = group[1] in VECTOR_COPY_GROUPS and group[0] < BATCHES - 1
             copy = nc.vector.tensor_copy if by_vector else nc.scalar.copy
             copy(
                 out=grouped_words[:, :count],

from contextlib import ExitStack

import concourse.mybir as mybir
from concourse.masks import make_identity

BF16 = mybir.dt.bfloat16
F32 = mybir.dt.float32
U32 = mybir.dt.uint32
U8 = mybir.dt.uint8
FP8X4 = mybir.dt.float8_e4m3fn_x4
ALU = mybir.AluOpType
ACT = mybir.ActivationFunctionType
AXIS = mybir.AxisListType

P = 128
PACK = 4
K_PASS = P * PACK
BANK = 512
BATCHES = 6
FEATURES = 512
KEYS = 1024
FIRST_QUERY = 128
QUERIES = KEYS - FIRST_QUERY
QUERY_TILES = QUERIES // P
TILES = BATCHES * QUERY_TILES
PAIR = 2
EPS = 1e-12
NEG = -1e15

LOAD_AHEAD = 10
SQUARE_AHEAD = 8
FLIP_AHEAD = 4
COPY_AHEAD = 3
QUANTISE_AHEAD = 2
VALUES_LOAD_AHEAD = (8, 13)
VALUES_REGROUP_AHEAD = (6, 11)
VALUES_QUANTISE_AHEAD = (4, 9)
RESIDUAL_LOAD_AHEAD = 8
DRAIN_TILES = 3
VECTOR_SQUARES = (0, 1)
VECTOR_COPY_GROUPS = (3, 7)

FLOPS = 2 * 2 * BATCHES * FEATURES * (384 * 512 + 512 * 1024)


def mx_widths(width):
    pieces = []
    start = 0
    for n in (512, 256, 128):
        while width - start >= n:
            pieces.append((start, n))
            start += n
    return pieces


def groups_due(n):
    if not 0 <= n < TILES:
        return []
    b, qi = divmod(n, QUERY_TILES)
    if qi == 0:
        return [(b, 0), (b, 1)]
    return [(b, qi + 1)]


def groups_at(s, ahead):
    first, later = ahead
    return [g for g in groups_due(s + first) if g[0] == 0] + [
        g for g in groups_due(s + later) if g[0] > 0
    ]


def tile_spatialangularattention_pa_t_kernel(tc, q_rows, k_rows, v_rows, out):
    nc = tc.nc
    with ExitStack() as stack:
        const = stack.enter_context(tc.tile_pool(name="const", bufs=1))
        raw_pool = stack.enter_context(tc.tile_pool(name="raw", bufs=12))
        junk_pool = stack.enter_context(tc.tile_pool(name="junk", bufs=2))
        row_pool = stack.enter_context(tc.tile_pool(name="rows", bufs=9))
        value_pool = stack.enter_context(tc.tile_pool(name="values", bufs=2))
        batch_pool = stack.enter_context(tc.tile_pool(name="batch", bufs=3))
        value_code_pool = stack.enter_context(tc.tile_pool(name="value_codes", bufs=4))
        stat_pool = stack.enter_context(tc.tile_pool(name="stats", bufs=6))
        work_pool = stack.enter_context(tc.tile_pool(name="work", bufs=4))
        flip_psum = stack.enter_context(tc.psum_pool(name="flip_psum", bufs=3))
        score_psum = stack.enter_context(tc.psum_pool(name="score_psum", bufs=4))
        out_psum = stack.enter_context(tc.psum_pool(name="out_psum", bufs=1))
        stack.enter_context(tc.manual_schedule())

        identity = const.tile([P, P], F32)
        make_identity(nc, identity[:])
        causal = const.tile([P, P], F32)
        nc.gpsimd.memset(causal[:], 0.0)
        nc.gpsimd.affine_select(
            out=causal[:],
            in_=causal[:],
            pattern=[[-1, P]],
            compare_op=ALU.is_ge,
            fill=NEG,
            base=0,
            channel_multiplier=1,
        )
        minus_half = const.tile([P, 2 * PAIR], F32)
        nc.vector.memset(minus_half[:], -0.5)

        e_rows = []
        for qi in range(QUERY_TILES):
            seen = (qi + 2) * P
            reach = K_PASS if seen <= K_PASS else KEYS
            e_tile = const.tile([P, reach], BF16, name="e_rows%d" % qi)
            if seen < reach:
                nc.vector.memset(e_tile[:, seen:], 0.0)
            e_rows.append(e_tile)

        batches = {}
        values = {}
        groups = {}
        norms = {}
        tiles = {}


        def open_batch(b):
            q_codes = batch_pool.tile([P, QUERIES], U32, align_bytes=64)
            q_scales = batch_pool.tile([P, QUERIES], U8, align_bytes=64)
            k_codes = batch_pool.tile([P, KEYS], U32, align_bytes=64)
            k_scales = batch_pool.tile([P, KEYS], U8, align_bytes=64)
            residual = batch_pool.tile([P, KEYS // P, FEATURES], BF16)
            batches[b] = {
                "q_codes": q_codes,
                "q_scales": q_scales,
                "k_codes": k_codes,
                "k_scales": k_scales,
                "residual": residual,
            }

        def load_rows(group):
            b, j = group
            if j == 0:
                open_batch(b)
            first = (j // 2) * PAIR * P
            source, kind, total = (k_rows, "k", KEYS) if j % 2 == 0 else (q_rows, "q", QUERIES)
            count = min(PAIR, (total - first) // P)
            rows = slice(first, first + count * P)
            raw = raw_pool.tile([P, PAIR, FEATURES], BF16)
            nc.sync.dma_start(
                out=raw[:, :count, :], in_=source[b, rows, :].rearrange("(t p) d -> p t d", p=P)
            )
            groups[group] = {
                "raw": raw,
                "count": count,
                "codes": batches[b][kind + "_codes"][:, rows],
                "scales": batches[b][kind + "_scales"][:, rows],
            }

        def load_values(group):
            b, j = group
            if j % 4 != 1:
                return
            g = j // 4
            first = g * K_PASS
            if g == 0:
                v_codes = value_code_pool.tile([P, 2 * FEATURES], U32, align_bytes=64)
                v_scales = value_code_pool.tile([P, 2 * FEATURES], U8, align_bytes=64)
                values[b] = {"codes": v_codes, "scales": v_scales}
            raw_values = value_pool.tile([P, PACK, FEATURES], BF16)
            nc.sync.dma_start(
                out=raw_values[:].rearrange("p (u e) d -> p u e d", e=2),
                in_=v_rows[b, first : first + K_PASS, :].rearrange("(u p e) d -> p u e d", p=P, e=2),
            )
            values[b][g] = {"raw": raw_values}

        def load_residual(group):
            b, j = group
            if j % 4 != 1:
                return
            g = j // 4
            first = g * K_PASS
            skip = max(FIRST_QUERY - first, 0) // P
            nc.sync.dma_start(
                out=batches[b]["residual"][:, g * PACK + skip : (g + 1) * PACK, :],
                in_=v_rows[b, first + skip * P : first + K_PASS, :].rearrange(
                    "(t p) d -> p t d", p=P
                ),
            )

        def square_sums(group):
            b, j = group
            state = groups[group]
            count = state["count"]
            if j % 2 == 0:
                square_sum = stat_pool.tile([P, 2 * PAIR], F32)
                norms[(b, j // 2)] = {"square_sum": square_sum}
            shared = norms[(b, j // 2)]
            unit = row_pool.tile([P, PAIR, FEATURES], BF16)
            state["unit"] = unit
            for t in range(count):
                column = PAIR * (j % 2) + t
                if group == VECTOR_SQUARES:
                    vector_squares = junk_pool.tile([P, FEATURES], F32)
                    nc.vector.scalar_tensor_tensor(
                        out=vector_squares[:],
                        in0=state["raw"][:, t, :],
                        scalar=1.0,
                        in1=state["raw"][:, t, :],
                        op0=ALU.mult,
                        op1=ALU.mult,
                        accum_out=shared["square_sum"][:, column : column + 1],
                    )
                else:
                    nc.scalar.activation(
                        out=unit[:, t, :],
                        in_=state["raw"][:, t, :],
                        func=ACT.Square,
                        accum_out=shared["square_sum"][:, column : column + 1],
                    )
            if j % 2 == 1:
                columns = PAIR + count
                floored = stat_pool.tile([P, 2 * PAIR], F32)
                nc.gpsimd.tensor_scalar_max(
                    out=floored[:, :columns],
                    in0=shared["square_sum"][:, :columns],
                    scalar1=EPS * EPS,
                )
                inv_norm = stat_pool.tile([P, 2 * PAIR], F32)
                nc.gpsimd.tensor_tensor(
                    out=inv_norm[:, :columns],
                    in0=floored[:, :columns],
                    in1=minus_half[:, :columns],
                    op=ALU.pow,
                )
                shared["inv_norm"] = inv_norm

        def normalise(group):
            b, j = group
            state = groups[group]
            for t in range(state["count"]):
                column = PAIR * (j % 2) + t
                nc.vector.tensor_scalar_mul(
                    out=state["unit"][:, t, :],
                    in0=state["raw"][:, t, :],
                    scalar1=norms[(b, j // 2)]["inv_norm"][:, column : column + 1],
                )

        def flip_rows(group):
            state = groups[group]
            flipped = flip_psum.tile([P, PAIR, 2, P], F32)
            for t in range(state["count"]):
                words = state["unit"][:, t, :].bitcast(F32)
                for u in range(2):
                    nc.tensor.transpose(
                        flipped[:, t, u, :], words[:, u * P : (u + 1) * P], identity[:]
                    )
            state["flipped"] = flipped

        def copy_rows(group):
            state = groups[group]
            count = state["count"]
            grouped = row_pool.tile([P, PAIR * FEATURES], BF16, align_bytes=64)
            grouped_words = grouped[:].bitcast(F32).rearrange("p (t r u) -> p t r u", t=PAIR, u=2)
            by_vector = group[1] in VECTOR_COPY_GROUPS and group[0] < BATCHES - 1
            copy = nc.vector.tensor_copy if by_vector else nc.scalar.copy
            copy(
                out=grouped_words[:, :count],
                in_=state["flipped"][:, :count].rearrange("p t u r -> p t r u"),
            )
            state["grouped"] = grouped

        def quantise_rows(group):
            state = groups[group]
            nc.vector.quantize_mx(
                out=state["codes"].bitcast(FP8X4),
                scales=state["scales"],
                in_=state["grouped"][:, : state["count"] * FEATURES],
            )

        def regroup_values(group):
            b, j = group
            if j % 4 != 1:
                return
            grouped_values = value_pool.tile([P, FEATURES, PACK], BF16, align_bytes=64)
            nc.vector.tensor_copy(
                out=grouped_values[:].rearrange("p (c i) s -> p c s i", i=4),
                in_=values[b][j // 4]["raw"][:].rearrange("p s (c i) -> p c s i", i=4),
            )
            values[b][j // 4]["grouped"] = grouped_values

        def quantise_values(group):
            b, j = group
            if j % 4 != 1:
                return
            columns = slice((j // 4) * FEATURES, (j // 4 + 1) * FEATURES)
            nc.vector.quantize_mx(
                out=values[b]["codes"][:, columns].bitcast(FP8X4),
                scales=values[b]["scales"][:, columns],
                in_=values[b][j // 4]["grouped"][:].rearrange("p d s -> p (d s)"),
            )


        def score(n):
            if not 0 <= n < TILES:
                return
            b, qi = divmod(n, QUERY_TILES)
            batch = batches[b]
            seen = (qi + 2) * P
            queries = slice(qi * P, (qi + 1) * P)
            banks = []
            for first in range(0, seen, BANK):
                bank = score_psum.tile([P, BANK], F32)
                for start, width in mx_widths(min(seen - first, BANK)):
                    keys = slice(first + start, first + start + width)
                    nc.tensor.matmul_mx(
                        out=bank[:, start : start + width],
                        lhsT=batch["q_codes"][:, queries].bitcast(FP8X4),
                        lhsT_scale=batch["q_scales"][:, queries],
                        rhs=batch["k_codes"][:, keys].bitcast(FP8X4),
                        rhs_scale=batch["k_scales"][:, keys],
                        start=True,
                        stop=True,
                    )
                banks.append(bank)
            tiles[n] = {"batch": batch, "b": b, "qi": qi, "seen": seen, "banks": banks}

        def piece_maxima(n):
            if not 0 <= n < TILES:
                return
            state = tiles[n]
            seen = state["seen"]
            masked = work_pool.tile([P, P + 2], F32)
            diagonal = (seen - P) % BANK
            nc.vector.tensor_tensor(
                out=masked[:, :P],
                in0=state["banks"][-1][:, diagonal : diagonal + P],
                in1=causal[:],
                op=ALU.add,
            )
            pieces = []
            for g, bank in enumerate(state["banks"]):
                open_keys = min(seen - P - g * BANK, BANK)
                if open_keys > 0:
                    pieces.append((g * BANK, bank[:, :open_keys]))
            for i, (first, piece) in enumerate(pieces):
                nc.vector.tensor_reduce(
                    out=masked[:, P + i : P + i + 1], in_=piece, axis=AXIS.X, op=ALU.max
                )
            state["masked"] = masked[:, : P + len(pieces)]
            pieces.append((seen - P, masked[:, :P]))
            state["pieces"] = pieces

        def negate_maximum(n):
            if not 0 <= n < TILES:
                return
            state = tiles[n]
            minus_max = stat_pool.tile([P, 1], F32)
            nc.vector.tensor_reduce(
                out=minus_max[:],
                in_=state["masked"],
                axis=AXIS.X,
                op=ALU.max,
                negate=True,
            )
            state["minus_max"] = minus_max

        def exponentials(n):
            if not 0 <= n < TILES:
                return
            state = tiles[n]
            piece_sum = stat_pool.tile([P, 3], F32)
            for i, (first, piece) in enumerate(state["pieces"]):
                nc.scalar.activation(
                    out=e_rows[state["qi"]][:, first : first + piece.shape[1]],
                    in_=piece,
                    func=ACT.Exp,
                    bias=state["minus_max"][:, 0:1],
                    scale=1.0,
                    accum_out=piece_sum[:, i : i + 1],
                )
            state["piece_sum"] = piece_sum

        def sum_pieces(n):
            if not 0 <= n < TILES:
                return
            state = tiles[n]
            count = len(state["pieces"])
            copied = stat_pool.tile([P, 3], F32)
            row_sum = stat_pool.tile([P, 1], F32)
            nc.scalar.activation(
                out=copied[:, :count],
                in_=state["piece_sum"][:, :count],
                func=ACT.Copy,
                accum_out=row_sum[:],
            )
            state["row_sum"] = row_sum

        def invert_sum(n):
            if not 0 <= n < TILES:
                return
            inv_sum = stat_pool.tile([P, 1], F32)
            nc.vector.reciprocal(out=inv_sum[:], in_=tiles[n]["row_sum"][:])
            tiles[n]["inv_sum"] = inv_sum

        def flip_e(n):
            if not 0 <= n < TILES:
                return
            e_tile = e_rows[tiles[n]["qi"]]
            flipped = flip_psum.tile([P, KEYS // (2 * P), P], F32)
            e_words = e_tile[:].bitcast(F32)
            for w in range(e_tile.shape[1] // (2 * P)):
                nc.tensor.transpose(flipped[:, w, :], e_words[:, w * P : (w + 1) * P], identity[:])
            tiles[n]["flipped"] = flipped
            tiles[n]["passes"] = e_tile.shape[1] // K_PASS

        def copy_e(n):
            if not 0 <= n < TILES:
                return
            passes = tiles[n]["passes"]
            grouped = work_pool.tile([P, KEYS], BF16, align_bytes=64)
            grouped_words = grouped[:].bitcast(F32).rearrange("p (g i u) -> p g i u", i=P, u=2)
            nc.scalar.copy(
                out=grouped_words[:, :passes],
                in_=tiles[n]["flipped"][:, : 2 * passes, :].rearrange("p (g u) i -> p g i u", u=2),
            )
            tiles[n]["grouped"] = grouped

        def quantise_e(n):
            if not 0 <= n < TILES:
                return
            passes = tiles[n]["passes"]
            e_codes = work_pool.tile([P, KEYS // PACK], U32, align_bytes=64)
            e_scales = work_pool.tile([P, KEYS // PACK], U8, align_bytes=64)
            nc.vector.quantize_mx(
                out=e_codes[:, : passes * P].bitcast(FP8X4),
                scales=e_scales[:, : passes * P],
                in_=tiles[n]["grouped"][:, : passes * K_PASS],
            )
            tiles[n]["e_codes"] = e_codes
            tiles[n]["e_scales"] = e_scales

        def mix_values(n):
            if not 0 <= n < TILES:
                return
            state = tiles[n]
            if n < TILES - DRAIN_TILES:
                mixed = out_psum.tile([P, FEATURES], F32)
            else:
                bank = score_psum.tile([P, BANK], F32)
                mixed = bank
            for g in range(state["passes"]):
                nc.tensor.matmul_mx(
                    out=mixed[:],
                    lhsT=state["e_codes"][:, g * P : (g + 1) * P].bitcast(FP8X4),
                    lhsT_scale=state["e_scales"][:, g * P : (g + 1) * P],
                    rhs=values[state["b"]]["codes"][:, g * FEATURES : (g + 1) * FEATURES].bitcast(FP8X4),
                    rhs_scale=values[state["b"]]["scales"][:, g * FEATURES : (g + 1) * FEATURES],
                    start=(g == 0),
                    stop=(g == state["passes"] - 1),
                )
            state["mixed"] = mixed

        def finish(n):
            if not 0 <= n < TILES:
                return
            state = tiles[n]
            qi = state["qi"]
            result = work_pool.tile([P, FEATURES], F32)
            nc.vector.scalar_tensor_tensor(
                out=result[:],
                in0=state["mixed"][:],
                scalar=state["inv_sum"][:, 0:1],
                in1=state["batch"]["residual"][:, qi + FIRST_QUERY // P, :],
                op0=ALU.mult,
                op1=ALU.add,
            )
            nc.sync.dma_start(out=out[state["b"], qi * P : (qi + 1) * P, :], in_=result[:])

        for s in range(-LOAD_AHEAD, TILES + 4):
            for group in groups_due(s + LOAD_AHEAD):
                load_rows(group)
            for group in groups_at(s, VALUES_LOAD_AHEAD):
                load_values(group)
            for group in groups_due(s + RESIDUAL_LOAD_AHEAD):
                load_residual(group)
            if s >= TILES:
                flip_e(s - 1)
            score(s + 1)
            mix_values(s - 4)
            for group in groups_due(s + SQUARE_AHEAD):
                square_sums(group)
            sum_pieces(s - 1)
            copy_e(s - 2)
            for group in groups_due(s + COPY_AHEAD):
                copy_rows(group)
            exponentials(s)
            for group in groups_due(s + FLIP_AHEAD):
                normalise(group)
            for group in groups_due(s + QUANTISE_AHEAD):
                quantise_rows(group)
            for group in groups_at(s, VALUES_QUANTISE_AHEAD):
                quantise_values(group)
            for group in groups_at(s, VALUES_REGROUP_AHEAD):
                regroup_values(group)
            quantise_e(s - 3)
            piece_maxima(s + 1)
            finish(s - 4)
            negate_maximum(s + 1)
            invert_sum(s - 1)
            if s < TILES:
                flip_e(s - 1)
            for group in groups_due(s + FLIP_AHEAD):
                flip_rows(group)
